import numpy as np
import ml_dtypes


def mxq(x, axis, fmt="e4m3"):
    dtype, down = {"e4m3": (ml_dtypes.float8_e4m3fn, 7), "e5m2": (ml_dtypes.float8_e5m2, 14)}[fmt]
    v = np.moveaxis(np.asarray(x, np.float32).astype(ml_dtypes.bfloat16).astype(np.float64), axis, -1)
    blocks = v.reshape(v.shape[:-1] + (-1, 32))
    amax = np.abs(blocks).max(-1, keepdims=True)
    byte = np.maximum(np.where(amax > 0, np.frexp(amax)[1] - 1 + 127, 0) - down, 1)
    scale = np.exp2(byte - 127.0)
    codes = (blocks / scale).astype(np.float32).astype(dtype).astype(np.float64)
    return np.moveaxis((codes * scale).reshape(v.shape), -1, axis)


WIDE = False


def mx_kscale(k):
    if not WIDE:
        return np.ones(k)
    levels = np.array([10, -10, 5, -5, 0])
    if k % 512:
        return np.exp2(np.random.permutation(np.resize(levels, k // 32))).repeat(32)
    a = np.empty((k // 512, 16))
    for p in range(k // 512):
        a[p, :8] = np.random.permutation(np.resize(levels, 8))
        for g in range(8):
            far = levels[np.abs(levels - a[p, g]) >= 10]
            a[p, g + 8] = far[np.random.randint(len(far))]
    return np.exp2(a.ravel()).repeat(32)


BF16 = ml_dtypes.bfloat16


def bf(x):
    return np.asarray(x, np.float32).astype(BF16)


def f64(x):
    return np.asarray(x).astype(np.float64)


B, IN, HID, PROJ, H, KC = 8192, 128, 512, 512, 4, 4
BH = HID // H
EPS = 1e-5


def silu(v):
    return v / (1.0 + np.exp(-v))


def groupnorm(v, w, b):
    r = v.reshape(B, H, BH)
    mu = r.mean(-1, keepdims=True)
    var = ((r - mu) ** 2).mean(-1, keepdims=True)
    rn = (r - mu) / np.sqrt(var + EPS)
    return rn.reshape(B, HID) * w + b


def setup_inputs():
    s, t = mx_kscale(PROJ), mx_kscale(HID)
    r = np.random.standard_normal
    return {"h_t": bf(r((B, HID)) * 0.5 / np.sqrt(HID)), "x_conv": bf(silu(r((B, PROJ))) * s),
            "x_right": bf(r((B, HID))), "x": bf(r((B, IN))),
            "gn_w": bf((1.0 + 0.1 * r(HID)) * t), "gn_b": bf(0.2 * r(HID) * t),
            "skip_w": bf(r((PROJ, HID)) * 1.5 / np.sqrt(PROJ) / s[:, None] * t[None, :]), "skip_b": bf(0.2 * r(HID) * t),
            "down_w": bf(r((HID, IN)) / np.sqrt(HID) / t[:, None]), "down_b": bf(0.2 * r(IN))}


def reference(h_t, x_conv, x_right, x, gn_w, gn_b, skip_w, skip_b, down_w, down_b):
    x_skip = f64(bf(mxq(f64(x_conv), 1, "e4m3") @ mxq(f64(skip_w), 0, "e4m3"))) + f64(skip_b)
    g = (groupnorm(f64(h_t), f64(gn_w), f64(gn_b)) + x_skip) * silu(f64(x_right))
    y = (mxq(g, 1, "e4m3") @ mxq(f64(down_w), 0, "e4m3")) + f64(down_b)
    return y + f64(x)

@@ -1,0 +1,413 @@
+from contextlib import ExitStack
+
+import concourse.mybir as mybir
+from concourse.masks import make_identity
+
+F32 = mybir.dt.float32
+BF16 = mybir.dt.bfloat16
+U32 = mybir.dt.uint32
+U8 = mybir.dt.uint8
+FP8X4 = mybir.dt.float8_e4m3fn_x4
+ALU = mybir.AluOpType
+ACT = mybir.ActivationFunctionType
+
+B, HID, PROJ, IN = 8192, 512, 512, 128
+EPS = 1e-5
+P = 128
+FLOPS = 2 * B * PROJ * HID + 2 * B * HID * IN
+
+BANK_DT = BF16
+
+NT = B // P
+JB = 4
+NBLK = NT // JB
+BT = 16
+NBATCH = NT // BT
+NPAIR = NT // 2
+
+LA_ST = BT + 7
+G_GROUPS = 3
+LEAD = 8
+H_BUFS = (LA_ST + LEAD) // JB + 2
+FIRST_SLOT = -LA_ST
+LAST_SLOT = NT + 3
+
+
+def tile_mlstmblock_pc_t_kernel(
+    tc, h_t, x_conv, x_right, x, gn_w, gn_b, skip_w, skip_b, down_w, down_b, out
+):
+    nc = tc.nc
+
+    h_v = h_t.rearrange("(b p j) n -> b p j n", p=P, j=JB)
+    xc_v = x_conv.rearrange("(b p j) n -> b p j n", p=P, j=JB)
+    xr_v = x_right.rearrange("(b p j) n -> b p j n", p=P, j=JB)
+    x_v = x.rearrange("(b p j) n -> b p j n", p=P, j=JB)
+    out_v = out.rearrange("(b p j) n -> b p j n", p=P, j=JB)
+
+    with ExitStack() as ctx:
+        const = ctx.enter_context(tc.tile_pool(name="const", bufs=1))
+        io = ctx.enter_context(tc.tile_pool(name="io", bufs=4))
+        work = ctx.enter_context(tc.tile_pool(name="work", bufs=3))
+        ps2 = ctx.enter_context(tc.psum_pool(name="ps2", bufs=2))
+        ps1 = ctx.enter_context(tc.psum_pool(name="ps1", bufs=1))
+        ctx.enter_context(tc.manual_schedule())
+
+        ident = const.tile([P, P], F32, name="ident", tag="ident")
+        w_raw = const.tile([P, 4, HID], BF16, name="w_raw", tag="w_raw")
+        w_grp = const.tile([P, 4 * HID], BF16, name="w_grp", tag="w_grp", align_bytes=64)
+        w_codes = const.tile([P, HID], U32, name="w_codes", tag="w_codes", align_bytes=64)
+        w_scales = const.tile([P, HID], U8, name="w_scales", tag="w_scales", align_bytes=64)
+        d_raw = const.tile([P, 4, IN], BF16, name="d_raw", tag="d_raw")
+        d_grp = const.tile([P, 4 * IN], BF16, name="d_grp", tag="d_grp", align_bytes=64)
+        d_codes = const.tile([P, IN], U32, name="d_codes", tag="d_codes", align_bytes=64)
+        d_scales = const.tile([P, IN], U8, name="d_scales", tag="d_scales", align_bytes=64)
+        gw_bf = const.tile([P, 4], BF16, name="gw_bf", tag="gw_bf")
+        gb_bf = const.tile([P, 4], BF16, name="gb_bf", tag="gb_bf")
+        sb_bf = const.tile([P, 4], BF16, name="sb_bf", tag="sb_bf")
+        w32 = const.tile([P, 4], F32, name="w32", tag="w32")
+        cb32 = const.tile([P, 4], F32, name="cb32", tag="cb32")
+        db4 = const.tile([P, JB, IN], BF16, name="db4", tag="db4")
+
+        tiles = {}
+
+        def load_h(b):
+            t = io.tile([P, JB, HID], BF16, name="h_blk", tag="h_blk", bufs=H_BUFS)
+            tiles["h", b] = t
+            nc.sync.dma_start(out=t[:], in_=h_v[b])
+
+        def load_xc(b):
+            t = io.tile([P, JB, PROJ], BF16, name="xc_blk", tag="xc_blk", bufs=4)
+            tiles["xc", b] = t
+            nc.sync.dma_start(out=t[:], in_=xc_v[b])
+
+        def load_xr(b):
+            t = io.tile([P, JB, HID], BF16, name="xr_blk", tag="xr_blk", bufs=4)
+            tiles["xr", b] = t
+            nc.sync.dma_start(out=t[:], in_=xr_v[b])
+
+        def load_x(b):
+            t = io.tile([P, JB, IN], BF16, name="x_blk", tag="x_blk", bufs=3)
+            tiles["x", b] = t
+            nc.sync.dma_start(out=t[:], in_=x_v[b])
+
+        def load_w():
+            nc.sync.dma_start(out=w_raw[:], in_=skip_w.rearrange("(p j) n -> p j n", j=4))
+
+        def load_vecs():
+            nc.sync.dma_start(out=gw_bf[:], in_=gn_w.rearrange("(p t) -> p t", t=4))
+            nc.sync.dma_start(out=gb_bf[:], in_=gn_b.rearrange("(p t) -> p t", t=4))
+            nc.sync.dma_start(out=sb_bf[:], in_=skip_b.rearrange("(p t) -> p t", t=4))
+
+        def load_d():
+            nc.sync.dma_start(out=d_raw[:], in_=down_w.rearrange("(p j) n -> p j n", j=4))
+
+        def load_db():
+            nc.sync.dma_start(out=db4[:, 0, :], in_=down_b.partition_broadcast(P))
+
+        def store(b):
+            nc.sync.dma_start(out=out_v[b], in_=tiles["o", b][:])
+
+        dmas = []
+        for b in range(NBLK):
+            dmas.append((JB * b - LA_ST, 0, load_h, b))
+            dmas.append((JB * b - 5, 1, load_xc, b))
+            dmas.append((JB * b - 3, 2, load_xr, b))
+            dmas.append((JB * b, 3, load_x, b))
+        dmas.append((-14, 0, load_w, None))
+        dmas.append((-8, 0, load_vecs, None))
+        dmas.append((-9, 5, load_d, None))
+        dmas.append((-2, 4, load_db, None))
+        dmas = sorted(dmas, key=lambda e: (e[0], e[1]))
+
+        def stats(i, a):
+            beta, r = divmod(i, BT)
+            if r == 0 and a == 0:
+                tiles["st", beta] = work.tile([P, BT * 12], F32, name="st", tag="st", bufs=3)
+            b, j = divmod(i, JB)
+            src = tiles["h", b][:, j, 256 * a : 256 * (a + 1)].rearrange("p (g c) -> p c g", g=2)
+            nc.vector.bn_stats(out=tiles["st", beta][:, 12 * r + 6 * a : 12 * r + 6 * a + 6], in_=src)
+
+        def rstd_v(beta):
+            t = work.tile([P, BT * 4], F32, name="rstd", tag="rstd", bufs=3)
+            tiles["rstd", beta] = t
+            nc.vector.reciprocal(out=t[:], in_=tiles["sd", beta][:])
+
+        def quant_w():
+            nc.vector.quantize_mx(out=w_codes[:].bitcast(FP8X4), scales=w_scales[:], in_=w_grp[:])
+
+        def quant_d():
+            nc.vector.quantize_mx(out=d_codes[:].bitcast(FP8X4), scales=d_scales[:], in_=d_grp[:])
+
+        def vecs_v():
+            nc.vector.tensor_copy(out=w32[:], in_=gw_bf[:])
+            nc.vector.tensor_tensor(out=cb32[:], in0=gb_bf[:], in1=sb_bf[:], op=ALU.add)
+
+        def db_v():
+            for j in range(1, JB):
+                nc.vector.tensor_copy(out=db4[:, j, :], in_=db4[:, 0, :])
+
+        def quant_xc(k):
+            c = work.tile([P, 2 * P], U32, name="xc_codes", tag="xc_codes", bufs=3, align_bytes=64)
+            s = work.tile([P, 2 * P], U8, name="xc_scales", tag="xc_scales", bufs=3, align_bytes=64)
+            tiles["xcq", k] = (c, s)
+            nc.vector.quantize_mx(out=c[:].bitcast(FP8X4), scales=s[:], in_=tiles["xcg", k][:])
+
+        def add_f(i):
+            t = work.tile([P, 4, P], F32, name="f_sum", tag="f_sum", bufs=3)
+            tiles["f", i] = t
+            nc.vector.tensor_tensor(out=t[:], in0=tiles["xsT", i][:], in1=tiles["hw", i][:], op=ALU.add)
+
+        def gate(i):
+            t = work.tile([P, 4 * P], BF16, name="g_bf", tag="g_bf", bufs=3, align_bytes=64)
+            tiles["g", i] = t
+            nc.vector.tensor_tensor(
+                out=t[:].rearrange("p (k t) -> p k t", t=4),
+                in0=tiles["f", i][:].rearrange("p t k -> p k t"),
+                in1=tiles["sT", i][:].rearrange("p t k -> p k t"),
+                op=ALU.mult,
+            )
+
+        def quant_g(i):
+            c = work.tile([P, P], U32, name="g_codes", tag="g_codes", bufs=4, align_bytes=64)
+            s = work.tile([P, P], U8, name="g_scales", tag="g_scales", bufs=4, align_bytes=64)
+            tiles["gq", i] = (c, s)
+            nc.vector.quantize_mx(out=c[:].bitcast(FP8X4), scales=s[:], in_=tiles["g", i][:])
+
+        def epilogue(b):
+            t = io.tile([P, JB, IN], F32, name="o_blk", tag="o_blk", bufs=3)
+            tiles["o", b] = t
+            nc.vector.tensor_tensor(out=t[:], in0=tiles["y", b][:], in1=tiles["xb", b][:], op=ALU.add)
+
+        def group_w():
+            nc.scalar.copy(
+                out=w_grp[:].rearrange("p (t m j) -> p t m j", t=4, j=4),
+                in_=w_raw[:].rearrange("p j (m t) -> p t m j", t=4),
+            )
+
+        def group_d():
+            nc.scalar.copy(
+                out=d_grp[:].rearrange("p (o j) -> p o j", j=4),
+                in_=d_raw[:].rearrange("p j o -> p o j"),
+            )
+
+        def sd_s(beta):
+            t = work.tile([P, BT * 4], F32, name="sd", tag="sd", bufs=3)
+            tiles["sd", beta] = t
+            m2 = tiles["st", beta][:].rearrange("p (n c) -> p n c", c=3)[:, :, 2]
+            nc.scalar.activation(out=t[:], in_=m2, func=ACT.Sqrt, bias=EPS, scale=1.0 / P)
+
+        def silu(i):
+            b, j = divmod(i, JB)
+            t = work.tile([P, 4, P], F32, name="s_perm", tag="s_perm", bufs=4)
+            tiles["sP", i] = t
+            nc.scalar.activation(
+                out=t[:], in_=tiles["xr", b][:, j, :].rearrange("p (c t) -> p t c", t=4), func=ACT.Silu
+            )
+
+        def normalise_s(i):
+            b, j = divmod(i, JB)
+            beta, r = divmod(i, BT)
+            for q in range(G_GROUPS, 4):
+                col = 4 * r + q
+                nc.scalar.activation(
+                    out=tiles["hnP", i][:, :, 32 * q : 32 * (q + 1)],
+                    in_=tiles["h", b][:, j, P * q : P * (q + 1)].rearrange("p (c t) -> p t c", t=4),
+                    func=ACT.Identity,
+                    bias=tiles["nmr", beta][:, col : col + 1],
+                    scale=tiles["rstd", beta][:, col : col + 1],
+                )
+
+        def copy_xc(k):
+            t = work.tile([P, 2 * 4 * P], BF16, name="xc_grp", tag="xc_grp", bufs=2, align_bytes=64)
+            tiles["xcg", k] = t
+            nc.scalar.copy(
+                out=t[:].bitcast(F32).rearrange("p (r k u) -> p r k u", r=2, u=2),
+                in_=tiles["xcT", k][:].rearrange("p r u k -> p r k u"),
+            )
+
+        def affine(i):
+            t = work.tile([P, 4, P], F32, name="hw", tag="hw", bufs=3)
+            tiles["hw", i] = t
+            for q in range(4):
+                nc.scalar.activation(
+                    out=t[:, q, :],
+                    in_=tiles["hnT", i][:, q, :],
+                    func=ACT.Identity,
+                    bias=cb32[:, q : q + 1],
+                    scale=w32[:, q : q + 1],
+                )
+
+        def negmu_g(beta):
+            t = work.tile([P, BT * 4], F32, name="negmu", tag="negmu", bufs=3)
+            tiles["negmu", beta] = t
+            mean = tiles["st", beta][:].rearrange("p (n c) -> p n c", c=3)[:, :, 1]
+            nc.gpsimd.tensor_scalar(out=t[:], in0=mean, scalar1=-1.0, scalar2=0.0, op0=ALU.mult, op1=ALU.add)
+
+        def normalise(i):
+            b, j = divmod(i, JB)
+            beta, r = divmod(i, BT)
+            t = work.tile([P, 4, P], F32, name="hn_perm", tag="hn_perm", bufs=4)
+            tiles["hnP", i] = t
+            for q in range(G_GROUPS):
+                col = 4 * r + q
+                nc.gpsimd.tensor_scalar(
+                    out=t[:, :, 32 * q : 32 * (q + 1)],
+                    in0=tiles["h", b][:, j, P * q : P * (q + 1)].rearrange("p (c t) -> p t c", t=4),
+                    scalar1=tiles["negmu", beta][:, col : col + 1],
+                    scalar2=tiles["rstd", beta][:, col : col + 1],
+                    op0=ALU.add,
+                    op1=ALU.mult,
+                )
+
+        def nmr_g(beta):
+            t = work.tile([P, BT * 4], F32, name="nmr", tag="nmr", bufs=3)
+            tiles["nmr", beta] = t
+            nc.gpsimd.tensor_tensor(out=t[:], in0=tiles["negmu", beta][:], in1=tiles["rstd", beta][:], op=ALU.mult)
+
+        def residual(b):
+            t = io.tile([P, JB, IN], F32, name="xb_blk", tag="xb_blk", bufs=3)
+            tiles["xb", b] = t
+            nc.gpsimd.tensor_tensor(out=t[:], in0=tiles["x", b][:], in1=db4[:], op=ALU.add)
+
+        def transpose_xc(k):
+            t = ps1.tile([P, 2, 2, P], F32, name="xcT", tag="xcT")
+            tiles["xcT", k] = t
+            for r in range(2):
+                b, j = divmod(2 * k + r, JB)
+                words = tiles["xc", b][:, j, :].bitcast(F32)
+                for u in range(2):
+                    nc.tensor.transpose(t[:, r, u, :], words[:, u::2], ident[:])
+
+        def transpose_hn(i):
+            t = ps2.tile([P, 4, P], F32, name="hnT", tag="hnT")
+            tiles["hnT", i] = t
+            for q in range(4):
+                nc.tensor.transpose(t[:, q, :], tiles["hnP", i][:, q, :], ident[:])
+
+        def transpose_s(i):
+            t = ps2.tile([P, 4, P], F32, name="sT", tag="sT")
+            tiles["sT", i] = t
+            for q in range(4):
+                nc.tensor.transpose(t[:, q, :], tiles["sP", i][:, q, :], ident[:])
+
+        def matmul_1(i):
+            t = ps2.tile([P, 4, P], BANK_DT, name="xsT", tag="xsT")
+            tiles["xsT", i] = t
+            k, r = divmod(i, 2)
+            c, s = tiles["xcq", k]
+            for q in range(4):
+                nc.tensor.matmul_mx(
+                    out=t[:, q, :],
+                    lhsT=w_codes[:, P * q : P * (q + 1)].bitcast(FP8X4),
+                    lhsT_scale=w_scales[:, P * q : P * (q + 1)],
+                    rhs=c[:, P * r : P * (r + 1)].bitcast(FP8X4),
+                    rhs_scale=s[:, P * r : P * (r + 1)],
+                    start=True,
+                    stop=True,
+                )
+
+        def matmul_2(i):
+            b, j = divmod(i, JB)
+            if j == 0:
+                tiles["y", b] = ps1.tile([P, JB, IN], F32, name="y", tag="y")
+            c, s = tiles["gq", i]
+            nc.tensor.matmul_mx(
+                out=tiles["y", b][:, j, :],
+                lhsT=c[:].bitcast(FP8X4),
+                lhsT_scale=s[:],
+                rhs=d_codes[:].bitcast(FP8X4),
+                rhs_scale=d_scales[:],
+                start=True,
+                stop=True,
+            )
+
+        def tile_ok(i):
+            return 0 <= i < NT
+
+        def due(slot, period, count):
+            n, rest = divmod(slot, period)
+            return n if rest == 0 and 0 <= n < count else None
+
+        make_identity(nc, ident[:])
+        n_dma = 0
+        for s in range(FIRST_SLOT, LAST_SLOT + 1):
+            while n_dma < len(dmas) and dmas[n_dma][0] - LEAD <= s:
+                e = dmas[n_dma]
+                if e[3] is None:
+                    e[2]()
+                else:
+                    e[2](e[3])
+                n_dma += 1
+            b = due(s - 7, JB, NBLK)
+            if b is not None:
+                store(b)
+
+            if tile_ok(s):
+                gate(s)
+            if tile_ok(s + LA_ST):
+                stats(s + LA_ST, 0)
+            b = due(s - 5, JB, NBLK)
+            if b is not None:
+                epilogue(b)
+            if tile_ok(s + 1):
+                add_f(s + 1)
+            if s == -8:
+                quant_w()
+            if s == -7:
+                vecs_v()
+            if s == -4:
+                quant_d()
+            if s == -3:
+                db_v()
+            k = due(s + 3, 2, NPAIR)
+            if k is not None:
+                quant_xc(k)
+            beta = due(s + 6, BT, NBATCH)
+            if beta is not None:
+                rstd_v(beta)
+            if tile_ok(s + LA_ST):
+                stats(s + LA_ST, 1)
+            if tile_ok(s):
+                quant_g(s)
+
+            if s == -13:
+                group_w()
+            if s == -9:
+                group_d()
+            if tile_ok(s + 2):
+                affine(s + 2)
+            k = due(s + 4, 2, NPAIR)
+            if k is not None:
+                copy_xc(k)
+            beta = due(s + 7, BT, NBATCH)
+            if beta is not None:
+                sd_s(beta)
+            if tile_ok(s + 4):
+                normalise_s(s + 4)
+            if tile_ok(s + 3):
+                silu(s + 3)
+
+            if beta is not None:
+                negmu_g(beta)
+            beta = due(s + 6, BT, NBATCH)
+            if beta is not None:
+                nmr_g(beta)
+            if tile_ok(s + 5):
+                normalise(s + 5)
+            b = due(s, JB, NBLK)
+            if b is not None:
+                residual(b)
+
+            if tile_ok(s + 3):
+                transpose_hn(s + 3)
+            k = due(s + 5, 2, NPAIR)
+            if k is not None:
+                transpose_xc(k)
+            if tile_ok(s + 1):
+                transpose_s(s + 1)
+            if tile_ok(s + 2):
+                matmul_1(s + 2)
+            if tile_ok(s - 2) and (s - 2) % JB == 0:
+                matmul_2(s - 2)
+            if tile_ok(s - 1) and (s - 1) % JB != 0:
+                matmul_2(s - 1)

@@ -25,10 +25,11 @@ BT = 16
 NBATCH = NT // BT
 NPAIR = NT // 2
 
-LA_ST = BT + 7
+O_NORM = 11
+LA_ST = BT + O_NORM + 2
 G_GROUPS = 3
 LEAD = 8
-H_BUFS = (LA_ST + LEAD) // JB + 2
+H_BUFS = (LA_ST + LEAD - O_NORM + 3) // JB + 2
 FIRST_SLOT = -LA_ST
 LAST_SLOT = NT + 3
 
@@ -110,11 +111,11 @@ def tile_mlstmblock_pc_t_kernel(
         dmas = []
         for b in range(NBLK):
             dmas.append((JB * b - LA_ST, 0, load_h, b))
-            dmas.append((JB * b - 5, 1, load_xc, b))
+            dmas.append((JB * b - 11, 1, load_xc, b))
             dmas.append((JB * b - 3, 2, load_xr, b))
             dmas.append((JB * b, 3, load_x, b))
-        dmas.append((-14, 0, load_w, None))
-        dmas.append((-8, 0, load_vecs, None))
+        dmas.append((-16, 0, load_w, None))
+        dmas.append((-10, 0, load_vecs, None))
         dmas.append((-9, 5, load_d, None))
         dmas.append((-2, 4, load_db, None))
         dmas = sorted(dmas, key=lambda e: (e[0], e[1]))
@@ -146,23 +147,25 @@ def tile_mlstmblock_pc_t_kernel(
             for j in range(1, JB):
                 nc.vector.tensor_copy(out=db4[:, j, :], in_=db4[:, 0, :])
 
-        def quant_xc(k):
-            c = work.tile([P, 2 * P], U32, name="xc_codes", tag="xc_codes", bufs=3, align_bytes=64)
-            s = work.tile([P, 2 * P], U8, name="xc_scales", tag="xc_scales", bufs=3, align_bytes=64)
-            tiles["xcq", k] = (c, s)
-            nc.vector.quantize_mx(out=c[:].bitcast(FP8X4), scales=s[:], in_=tiles["xcg", k][:])
+        def quant_xc(b):
+            c = work.tile([P, JB * P], U32, name="xc_codes", tag="xc_codes", bufs=2, align_bytes=64)
+            s = work.tile([P, JB * P], U8, name="xc_scales", tag="xc_scales", bufs=2, align_bytes=64)
+            tiles["xcq", b] = (c, s)
+            nc.vector.quantize_mx(out=c[:].bitcast(FP8X4), scales=s[:], in_=tiles["xcg", b][:])
 
-        def add_f(i):
-            t = work.tile([P, 4, P], F32, name="f_sum", tag="f_sum", bufs=3)
-            tiles["f", i] = t
-            nc.vector.tensor_tensor(out=t[:], in0=tiles["xsT", i][:], in1=tiles["hw", i][:], op=ALU.add)
+        def add_f(u):
+            b, t = divmod(u, 4)
+            if t == 0:
+                tiles["f", b] = work.tile([P, 4, JB, P], F32, name="f_sum", tag="f_sum", bufs=2)
+            nc.vector.tensor_tensor(out=tiles["f", b][:, t, :, :], in0=tiles["xsT", u][:], in1=tiles["hw", u][:], op=ALU.add)
 
         def gate(i):
+            b, j = divmod(i, JB)
             t = work.tile([P, 4 * P], BF16, name="g_bf", tag="g_bf", bufs=3, align_bytes=64)
             tiles["g", i] = t
             nc.vector.tensor_tensor(
                 out=t[:].rearrange("p (k t) -> p k t", t=4),
-                in0=tiles["f", i][:].rearrange("p t k -> p k t"),
+                in0=tiles["f", b][:, :, j, :].rearrange("p t k -> p k t"),
                 in1=tiles["sT", i][:].rearrange("p t k -> p k t"),
                 op=ALU.mult,
             )
@@ -218,24 +221,21 @@ def tile_mlstmblock_pc_t_kernel(
                 )
 
         def copy_xc(k):
-            t = work.tile([P, 2 * 4 * P], BF16, name="xc_grp", tag="xc_grp", bufs=2, align_bytes=64)
-            tiles["xcg", k] = t
+            b, half = divmod(k, 2)
+            if half == 0:
+                tiles["xcg", b] = work.tile([P, JB * 4 * P], BF16, name="xc_grp", tag="xc_grp", bufs=2, align_bytes=64)
             nc.scalar.copy(
-                out=t[:].bitcast(F32).rearrange("p (r k u) -> p r k u", r=2, u=2),
+                out=tiles["xcg", b][:, 8 * P * half : 8 * P * (half + 1)].bitcast(F32).rearrange("p (r k u) -> p r k u", r=2, u=2),
                 in_=tiles["xcT", k][:].rearrange("p r u k -> p r k u"),
             )
 
-        def affine(i):
-            t = work.tile([P, 4, P], F32, name="hw", tag="hw", bufs=3)
-            tiles["hw", i] = t
-            for q in range(4):
-                nc.scalar.activation(
-                    out=t[:, q, :],
-                    in_=tiles["hnT", i][:, q, :],
-                    func=ACT.Identity,
-                    bias=cb32[:, q : q + 1],
-                    scale=w32[:, q : q + 1],
-                )
+        def affine(u):
+            t = u % 4
+            hw = work.tile([P, JB, P], F32, name="hw", tag="hw", bufs=3)
+            tiles["hw", u] = hw
+            nc.scalar.activation(
+                out=hw[:], in_=tiles["hnT", u][:], func=ACT.Identity, bias=cb32[:, t : t + 1], scale=w32[:, t : t + 1]
+            )
 
         def negmu_g(beta):
             t = work.tile([P, BT * 4], F32, name="negmu", tag="negmu", bufs=3)
@@ -246,7 +246,7 @@ def tile_mlstmblock_pc_t_kernel(
         def normalise(i):
             b, j = divmod(i, JB)
             beta, r = divmod(i, BT)
-            t = work.tile([P, 4, P], F32, name="hn_perm", tag="hn_perm", bufs=4)
+            t = work.tile([P, 4, P], F32, name="hn_perm", tag="hn_perm", bufs=12)
             tiles["hnP", i] = t
             for q in range(G_GROUPS):
                 col = 4 * r + q
@@ -278,11 +278,12 @@ def tile_mlstmblock_pc_t_kernel(
                 for u in range(2):
                     nc.tensor.transpose(t[:, r, u, :], words[:, u::2], ident[:])
 
-        def transpose_hn(i):
-            t = ps2.tile([P, 4, P], F32, name="hnT", tag="hnT")
-            tiles["hnT", i] = t
-            for q in range(4):
-                nc.tensor.transpose(t[:, q, :], tiles["hnP", i][:, q, :], ident[:])
+        def transpose_hn(u):
+            b, t = divmod(u, 4)
+            bank = ps2.tile([P, JB, P], F32, name="hnT", tag="hnT")
+            tiles["hnT", u] = bank
+            for j in range(JB):
+                nc.tensor.transpose(bank[:, j, :], tiles["hnP", JB * b + j][:, t, :], ident[:])
 
         def transpose_s(i):
             t = ps2.tile([P, 4, P], F32, name="sT", tag="sT")
@@ -290,21 +291,20 @@ def tile_mlstmblock_pc_t_kernel(
             for q in range(4):
                 nc.tensor.transpose(t[:, q, :], tiles["sP", i][:, q, :], ident[:])
 
-        def matmul_1(i):
-            t = ps2.tile([P, 4, P], BANK_DT, name="xsT", tag="xsT")
-            tiles["xsT", i] = t
-            k, r = divmod(i, 2)
-            c, s = tiles["xcq", k]
-            for q in range(4):
-                nc.tensor.matmul_mx(
-                    out=t[:, q, :],
-                    lhsT=w_codes[:, P * q : P * (q + 1)].bitcast(FP8X4),
-                    lhsT_scale=w_scales[:, P * q : P * (q + 1)],
-                    rhs=c[:, P * r : P * (r + 1)].bitcast(FP8X4),
-                    rhs_scale=s[:, P * r : P * (r + 1)],
-                    start=True,
-                    stop=True,
-                )
+        def matmul_1(u):
+            b, t = divmod(u, 4)
+            bank = ps2.tile([P, JB, P], BANK_DT, name="xsT", tag="xsT")
+            tiles["xsT", u] = bank
+            c, s = tiles["xcq", b]
+            nc.tensor.matmul_mx(
+                out=bank[:].rearrange("p j k -> p (j k)"),
+                lhsT=w_codes[:, P * t : P * (t + 1)].bitcast(FP8X4),
+                lhsT_scale=w_scales[:, P * t : P * (t + 1)],
+                rhs=c[:].bitcast(FP8X4),
+                rhs_scale=s[:],
+                start=True,
+                stop=True,
+            )
 
         def matmul_2(i):
             b, j = divmod(i, JB)
@@ -349,20 +349,20 @@ def tile_mlstmblock_pc_t_kernel(
             b = due(s - 5, JB, NBLK)
             if b is not None:
                 epilogue(b)
-            if tile_ok(s + 1):
-                add_f(s + 1)
-            if s == -8:
+            if tile_ok(s + 4):
+                add_f(s + 4)
+            if s == -10:
                 quant_w()
-            if s == -7:
+            if s == -9:
                 vecs_v()
             if s == -4:
                 quant_d()
             if s == -3:
                 db_v()
-            k = due(s + 3, 2, NPAIR)
-            if k is not None:
-                quant_xc(k)
-            beta = due(s + 6, BT, NBATCH)
+            b = due(s + 7, JB, NBLK)
+            if b is not None:
+                quant_xc(b)
+            beta = due(s + O_NORM + 1, BT, NBATCH)
             if beta is not None:
                 rstd_v(beta)
             if tile_ok(s + LA_ST):
@@ -370,43 +370,43 @@ def tile_mlstmblock_pc_t_kernel(
             if tile_ok(s):
                 quant_g(s)
 
-            if s == -13:
+            if s == -15:
                 group_w()
             if s == -9:
                 group_d()
-            if tile_ok(s + 2):
-                affine(s + 2)
-            k = due(s + 4, 2, NPAIR)
+            if tile_ok(s + 5):
+                affine(s + 5)
+            k = due(s + 10, 2, NPAIR)
             if k is not None:
                 copy_xc(k)
-            beta = due(s + 7, BT, NBATCH)
+            beta = due(s + O_NORM + 2, BT, NBATCH)
             if beta is not None:
                 sd_s(beta)
-            if tile_ok(s + 4):
-                normalise_s(s + 4)
+            if tile_ok(s + O_NORM - 1):
+                normalise_s(s + O_NORM - 1)
             if tile_ok(s + 3):
                 silu(s + 3)
 
             if beta is not None:
                 negmu_g(beta)
-            beta = due(s + 6, BT, NBATCH)
+            beta = due(s + O_NORM + 1, BT, NBATCH)
             if beta is not None:
                 nmr_g(beta)
-            if tile_ok(s + 5):
-                normalise(s + 5)
+            if tile_ok(s + O_NORM):
+                normalise(s + O_NORM)
             b = due(s, JB, NBLK)
             if b is not None:
                 residual(b)
 
-            if tile_ok(s + 3):
-                transpose_hn(s + 3)
-            k = due(s + 5, 2, NPAIR)
+            if tile_ok(s + 6):
+                transpose_hn(s + 6)
+            k = due(s + 11, 2, NPAIR)
             if k is not None:
                 transpose_xc(k)
             if tile_ok(s + 1):
                 transpose_s(s + 1)
-            if tile_ok(s + 2):
-                matmul_1(s + 2)
+            if tile_ok(s + 5):
+                matmul_1(s + 5)
             if tile_ok(s - 2) and (s - 2) % JB == 0:
                 matmul_2(s - 2)
             if tile_ok(s - 1) and (s - 1) % JB != 0:

@@ -164,9 +164,9 @@ def tile_mlstmblock_pc_t_kernel(
             t = work.tile([P, 4 * P], BF16, name="g_bf", tag="g_bf", bufs=3, align_bytes=64)
             tiles["g", i] = t
             nc.vector.tensor_tensor(
-                out=t[:].rearrange("p (k t) -> p k t", t=4),
-                in0=tiles["f", b][:, :, j, :].rearrange("p t k -> p k t"),
-                in1=tiles["sT", i][:].rearrange("p t k -> p k t"),
+                out=t[:].rearrange("p (c i t) -> p c t i", i=4, t=4),
+                in0=tiles["f", b][:, :, j, :].rearrange("p t (c i) -> p c t i", i=4),
+                in1=tiles["sT", i][:].rearrange("p t (c i) -> p c t i", i=4),
                 op=ALU.mult,
             )
 

@@ -27,7 +27,7 @@ NPAIR = NT // 2
 
 O_NORM = 11
 LA_ST = BT + O_NORM + 2
-G_GROUPS = 3
+G_GROUPS = 2
 LEAD = 8
 H_BUFS = (LA_ST + LEAD - O_NORM + 3) // JB + 2
 FIRST_SLOT = -LA_ST

@@ -27,11 +27,13 @@ NPAIR = NT // 2
 
 O_NORM = 11
 LA_ST = BT + O_NORM + 2
-G_GROUPS = 2
+G_GROUPS = (2, 3)
 LEAD = 8
 H_BUFS = (LA_ST + LEAD - O_NORM + 3) // JB + 2
+S_STAT_TILES = 24
+B_SWITCH = (NT - LA_ST) // JB
 FIRST_SLOT = -LA_ST
-LAST_SLOT = NT + 3
+LAST_SLOT = NT + 4
 
 
 def tile_mlstmblock_pc_t_kernel(
@@ -68,6 +70,7 @@ def tile_mlstmblock_pc_t_kernel(
         w32 = const.tile([P, 4], F32, name="w32", tag="w32")
         cb32 = const.tile([P, 4], F32, name="cb32", tag="cb32")
         db4 = const.tile([P, JB, IN], BF16, name="db4", tag="db4")
+        warm = const.tile([P, 2], F32, name="warm", tag="warm")
 
         tiles = {}
 
@@ -116,14 +119,22 @@ def tile_mlstmblock_pc_t_kernel(
             dmas.append((JB * b, 3, load_x, b))
         dmas.append((-16, 0, load_w, None))
         dmas.append((-10, 0, load_vecs, None))
-        dmas.append((-9, 5, load_d, None))
+        dmas.append((-14, 5, load_d, None))
         dmas.append((-2, 4, load_db, None))
         dmas = sorted(dmas, key=lambda e: (e[0], e[1]))
+
+        def g_groups(i):
+            return 1 if i < JB else G_GROUPS[i % 2]
+
+        def on_scalar(i):
+            return i % JB == JB - 1 and i < S_STAT_TILES
 
         def stats(i, a):
             beta, r = divmod(i, BT)
             if r == 0 and a == 0:
                 tiles["st", beta] = work.tile([P, BT * 12], F32, name="st", tag="st", bufs=3)
+            if on_scalar(i):
+                return
             b, j = divmod(i, JB)
             src = tiles["h", b][:, j, 256 * a : 256 * (a + 1)].rearrange("p (g c) -> p c g", g=2)
             nc.vector.bn_stats(out=tiles["st", beta][:, 12 * r + 6 * a : 12 * r + 6 * a + 6], in_=src)
@@ -176,22 +187,32 @@ def tile_mlstmblock_pc_t_kernel(
             tiles["gq", i] = (c, s)
             nc.vector.quantize_mx(out=c[:].bitcast(FP8X4), scales=s[:], in_=tiles["g", i][:])
 
-        def epilogue(b):
-            t = io.tile([P, JB, IN], F32, name="o_blk", tag="o_blk", bufs=3)
-            tiles["o", b] = t
-            nc.vector.tensor_tensor(out=t[:], in0=tiles["y", b][:], in1=tiles["xb", b][:], op=ALU.add)
 
-        def group_w():
-            nc.scalar.copy(
-                out=w_grp[:].rearrange("p (t m j) -> p t m j", t=4, j=4),
-                in_=w_raw[:].rearrange("p j (m t) -> p t m j", t=4),
-            )
+        def preload_sqrt():
+            nc.scalar.activation(out=warm[:, 1:2], in_=warm[:, 0:1], func=ACT.Sqrt)
 
-        def group_d():
-            nc.scalar.copy(
-                out=d_grp[:].rearrange("p (o j) -> p o j", j=4),
-                in_=d_raw[:].rearrange("p j o -> p o j"),
-            )
+        def stats_s(i):
+            beta, r = divmod(i, BT)
+            b, j = divmod(i, JB)
+            st = tiles["st", beta]
+            for sweep in range(2):
+                for q in range(4):
+                    col = 12 * r + 3 * q
+                    junk = work.tile([P, P], BF16, name="junk", tag="junk", bufs=2)
+                    src = tiles["h", b][:, j, P * q : P * (q + 1)]
+                    if sweep == 0:
+                        nc.scalar.activation(
+                            out=junk[:], in_=src, func=ACT.Identity, scale=1.0 / P, accum_out=st[:, col + 1 : col + 2]
+                        )
+                    else:
+                        nc.scalar.activation(
+                            out=junk[:],
+                            in_=src,
+                            func=ACT.Square,
+                            bias=st[:, col + 1 : col + 2],
+                            scale=-1.0,
+                            accum_out=st[:, col + 2 : col + 3],
+                        )
 
         def sd_s(beta):
             t = work.tile([P, BT * 4], F32, name="sd", tag="sd", bufs=3)
@@ -210,7 +231,7 @@ def tile_mlstmblock_pc_t_kernel(
         def normalise_s(i):
             b, j = divmod(i, JB)
             beta, r = divmod(i, BT)
-            for q in range(G_GROUPS, 4):
+            for q in range(g_groups(i), 4):
                 col = 4 * r + q
                 nc.scalar.activation(
                     out=tiles["hnP", i][:, :, 32 * q : 32 * (q + 1)],
@@ -237,6 +258,41 @@ def tile_mlstmblock_pc_t_kernel(
                 out=hw[:], in_=tiles["hnT", u][:], func=ACT.Identity, bias=cb32[:, t : t + 1], scale=w32[:, t : t + 1]
             )
 
+        def epilogue_v(b):
+            t = io.tile([P, JB, IN], F32, name="o_blk", tag="o_blk", bufs=3)
+            tiles["o", b] = t
+            nc.vector.tensor_tensor(out=t[:], in0=tiles["y", b][:], in1=tiles["xb", b][:], op=ALU.add)
+
+        def copy_y(b):
+            t = io.tile([P, JB, IN], F32, name="y_sb", tag="y_sb", bufs=3)
+            tiles["ysb", b] = t
+            nc.scalar.copy(out=t[:], in_=tiles["y", b][:])
+
+        def group_w():
+            nc.gpsimd.tensor_scalar(
+                out=w_grp[:].rearrange("p (t m j) -> p t m j", t=4, j=4),
+                in0=w_raw[:].rearrange("p j (m t) -> p t m j", t=4),
+                scalar1=1.0,
+                scalar2=0.0,
+                op0=ALU.mult,
+                op1=ALU.add,
+            )
+
+        def group_d():
+            nc.gpsimd.tensor_scalar(
+                out=d_grp[:].rearrange("p (o j) -> p o j", j=4),
+                in0=d_raw[:].rearrange("p j o -> p o j"),
+                scalar1=1.0,
+                scalar2=0.0,
+                op0=ALU.mult,
+                op1=ALU.add,
+            )
+
+        def epilogue(b):
+            t = io.tile([P, JB, IN], F32, name="o_blk", tag="o_blk", bufs=3)
+            tiles["o", b] = t
+            nc.gpsimd.tensor_tensor(out=t[:], in0=tiles["ysb", b][:], in1=tiles["xb", b][:], op=ALU.add)
+
         def negmu_g(beta):
             t = work.tile([P, BT * 4], F32, name="negmu", tag="negmu", bufs=3)
             tiles["negmu", beta] = t
@@ -248,7 +304,7 @@ def tile_mlstmblock_pc_t_kernel(
             beta, r = divmod(i, BT)
             t = work.tile([P, 4, P], F32, name="hn_perm", tag="hn_perm", bufs=12)
             tiles["hnP", i] = t
-            for q in range(G_GROUPS):
+            for q in range(g_groups(i)):
                 col = 4 * r + q
                 nc.gpsimd.tensor_scalar(
                     out=t[:, :, 32 * q : 32 * (q + 1)],
@@ -328,6 +384,8 @@ def tile_mlstmblock_pc_t_kernel(
             n, rest = divmod(slot, period)
             return n if rest == 0 and 0 <= n < count else None
 
+        nc.gpsimd.memset(warm[:, 0:1], 1.0)
+        preload_sqrt()
         make_identity(nc, ident[:])
         n_dma = 0
         for s in range(FIRST_SLOT, LAST_SLOT + 1):
@@ -338,7 +396,7 @@ def tile_mlstmblock_pc_t_kernel(
                 else:
                     e[2](e[3])
                 n_dma += 1
-            b = due(s - 7, JB, NBLK)
+            b = due(s - 8, JB, NBLK)
             if b is not None:
                 store(b)
 
@@ -347,8 +405,8 @@ def tile_mlstmblock_pc_t_kernel(
             if tile_ok(s + LA_ST):
                 stats(s + LA_ST, 0)
             b = due(s - 5, JB, NBLK)
-            if b is not None:
-                epilogue(b)
+            if b is not None and b >= B_SWITCH:
+                epilogue_v(b)
             if tile_ok(s + 4):
                 add_f(s + 4)
             if s == -10:
@@ -370,10 +428,8 @@ def tile_mlstmblock_pc_t_kernel(
             if tile_ok(s):
                 quant_g(s)
 
-            if s == -15:
-                group_w()
-            if s == -9:
-                group_d()
+            if tile_ok(s + LA_ST) and on_scalar(s + LA_ST):
+                stats_s(s + LA_ST)
             if tile_ok(s + 5):
                 affine(s + 5)
             k = due(s + 10, 2, NPAIR)
@@ -386,7 +442,17 @@ def tile_mlstmblock_pc_t_kernel(
                 normalise_s(s + O_NORM - 1)
             if tile_ok(s + 3):
                 silu(s + 3)
+            b = due(s - 5, JB, NBLK)
+            if b is not None and b < B_SWITCH:
+                copy_y(b)
 
+            if s == -15:
+                group_w()
+            if s == -14:
+                group_d()
+            b = due(s - 6, JB, NBLK)
+            if b is not None and b < B_SWITCH:
+                epilogue(b)
             if beta is not None:
                 negmu_g(beta)
             beta = due(s + O_NORM + 1, BT, NBATCH)

@@ -167,8 +167,13 @@ def tile_mlstmblock_pc_t_kernel(
         def add_f(u):
             b, t = divmod(u, 4)
             if t == 0:
-                tiles["f", b] = work.tile([P, 4, JB, P], F32, name="f_sum", tag="f_sum", bufs=2)
-            nc.vector.tensor_tensor(out=tiles["f", b][:, t, :, :], in0=tiles["xsT", u][:], in1=tiles["hw", u][:], op=ALU.add)
+                tiles["f", b] = work.tile([P, JB, P // 4, 4, 4], F32, name="f_sum", tag="f_sum", bufs=2)
+            nc.vector.tensor_tensor(
+                out=tiles["f", b][:, :, :, t, :],
+                in0=tiles["xsT", u][:].rearrange("p j (c i) -> p j c i", i=4),
+                in1=tiles["hw", u][:].rearrange("p j (c i) -> p j c i", i=4),
+                op=ALU.add,
+            )
 
         def gate(i):
             b, j = divmod(i, JB)
@@ -176,7 +181,7 @@ def tile_mlstmblock_pc_t_kernel(
             tiles["g", i] = t
             nc.vector.tensor_tensor(
                 out=t[:].rearrange("p (c i t) -> p c t i", i=4, t=4),
-                in0=tiles["f", b][:, :, j, :].rearrange("p t (c i) -> p c t i", i=4),
+                in0=tiles["f", b][:, j, :, :, :],
                 in1=tiles["sT", i][:].rearrange("p t (c i) -> p c t i", i=4),
                 op=ALU.mult,
             )

@@ -30,8 +30,9 @@ LA_ST = BT + O_NORM + 2
 G_GROUPS = (2, 3)
 LEAD = 8
 H_BUFS = (LA_ST + LEAD - O_NORM + 3) // JB + 2
-S_STAT_TILES = 24
+S_STAT_TILES = 16
 B_SWITCH = (NT - LA_ST) // JB
+B_BACK = 12
 FIRST_SLOT = -LA_ST
 LAST_SLOT = NT + 4
 
@@ -125,6 +126,9 @@ def tile_mlstmblock_pc_t_kernel(
 
         def g_groups(i):
             return 1 if i < JB else G_GROUPS[i % 2]
+
+        def on_vector(b):
+            return B_SWITCH <= b < B_BACK or b == NBLK - 1
 
         def on_scalar(i):
             return i % JB == JB - 1 and i < S_STAT_TILES
@@ -410,7 +414,7 @@ def tile_mlstmblock_pc_t_kernel(
             if tile_ok(s + LA_ST):
                 stats(s + LA_ST, 0)
             b = due(s - 5, JB, NBLK)
-            if b is not None and b >= B_SWITCH:
+            if b is not None and on_vector(b):
                 epilogue_v(b)
             if tile_ok(s + 4):
                 add_f(s + 4)
@@ -448,7 +452,7 @@ def tile_mlstmblock_pc_t_kernel(
             if tile_ok(s + 3):
                 silu(s + 3)
             b = due(s - 5, JB, NBLK)
-            if b is not None and b < B_SWITCH:
+            if b is not None and not on_vector(b):
                 copy_y(b)
 
             if s == -15:
@@ -456,7 +460,7 @@ def tile_mlstmblock_pc_t_kernel(
             if s == -14:
                 group_d()
             b = due(s - 6, JB, NBLK)
-            if b is not None and b < B_SWITCH:
+            if b is not None and not on_vector(b):
                 epilogue(b)
             if beta is not None:
                 negmu_g(beta)

from contextlib import ExitStack

import concourse.mybir as mybir
from concourse.masks import make_identity

F32 = mybir.dt.float32
BF16 = mybir.dt.bfloat16
U32 = mybir.dt.uint32
U8 = mybir.dt.uint8
FP8X4 = mybir.dt.float8_e4m3fn_x4
ALU = mybir.AluOpType
ACT = mybir.ActivationFunctionType

B, HID, PROJ, IN = 8192, 512, 512, 128
EPS = 1e-5
P = 128
FLOPS = 2 * B * PROJ * HID + 2 * B * HID * IN

BANK_DT = BF16

NT = B // P
JB = 4
NBLK = NT // JB
BT = 16
NBATCH = NT // BT
NPAIR = NT // 2

O_NORM = 11
LA_ST = BT + O_NORM + 2
G_GROUPS = (2, 3)
LEAD = 8
H_BUFS = (LA_ST + LEAD - O_NORM + 3) // JB + 2
S_STAT_TILES = 16
B_SWITCH = (NT - LA_ST) // JB
B_BACK = 12
FIRST_SLOT = -LA_ST
LAST_SLOT = NT + 4


def tile_mlstmblock_pc_t_kernel(
    tc, h_t, x_conv, x_right, x, gn_w, gn_b, skip_w, skip_b, down_w, down_b, out
):
    nc = tc.nc

    h_v = h_t.rearrange("(b p j) n -> b p j n", p=P, j=JB)
    xc_v = x_conv.rearrange("(b p j) n -> b p j n", p=P, j=JB)
    xr_v = x_right.rearrange("(b p j) n -> b p j n", p=P, j=JB)
    x_v = x.rearrange("(b p j) n -> b p j n", p=P, j=JB)
    out_v = out.rearrange("(b p j) n -> b p j n", p=P, j=JB)

    with ExitStack() as ctx:
        const = ctx.enter_context(tc.tile_pool(name="const", bufs=1))
        io = ctx.enter_context(tc.tile_pool(name="io", bufs=4))
        work = ctx.enter_context(tc.tile_pool(name="work", bufs=3))
        ps2 = ctx.enter_context(tc.psum_pool(name="ps2", bufs=2))
        ps1 = ctx.enter_context(tc.psum_pool(name="ps1", bufs=1))
        ctx.enter_context(tc.manual_schedule())

        ident = const.tile([P, P], F32, name="ident", tag="ident")
        w_raw = const.tile([P, 4, HID], BF16, name="w_raw", tag="w_raw")
        w_grp = const.tile([P, 4 * HID], BF16, name="w_grp", tag="w_grp", align_bytes=64)
        w_codes = const.tile([P, HID], U32, name="w_codes", tag="w_codes", align_bytes=64)
        w_scales = const.tile([P, HID], U8, name="w_scales", tag="w_scales", align_bytes=64)
        d_raw = const.tile([P, 4, IN], BF16, name="d_raw", tag="d_raw")
        d_grp = const.tile([P, 4 * IN], BF16, name="d_grp", tag="d_grp", align_bytes=64)
        d_codes = const.tile([P, IN], U32, name="d_codes", tag="d_codes", align_bytes=64)
        d_scales = const.tile([P, IN], U8, name="d_scales", tag="d_scales", align_bytes=64)
        gw_bf = const.tile([P, 4], BF16, name="gw_bf", tag="gw_bf")
        gb_bf = const.tile([P, 4], BF16, name="gb_bf", tag="gb_bf")
        sb_bf = const.tile([P, 4], BF16, name="sb_bf", tag="sb_bf")
        w32 = const.tile([P, 4], F32, name="w32", tag="w32")
        cb32 = const.tile([P, 4], F32, name="cb32", tag="cb32")
        db4 = const.tile([P, JB, IN], BF16, name="db4", tag="db4")
        warm = const.tile([P, 2], F32, name="warm", tag="warm")

        tiles = {}

        def load_h(b):
            t = io.tile([P, JB, HID], BF16, name="h_blk", tag="h_blk", bufs=H_BUFS)
            tiles["h", b] = t
            nc.sync.dma_start(out=t[:], in_=h_v[b])

        def load_xc(b):
            t = io.tile([P, JB, PROJ], BF16, name="xc_blk", tag="xc_blk", bufs=4)
            tiles["xc", b] = t
            nc.sync.dma_start(out=t[:], in_=xc_v[b])

        def load_xr(b):
            t = io.tile([P, JB, HID], BF16, name="xr_blk", tag="xr_blk", bufs=4)
            tiles["xr", b] = t
            nc.sync.dma_start(out=t[:], in_=xr_v[b])

        def load_x(b):
            t = io.tile([P, JB, IN], BF16, name="x_blk", tag="x_blk", bufs=3)
            tiles["x", b] = t
            nc.sync.dma_start(out=t[:], in_=x_v[b])

        def load_w():
            nc.sync.dma_start(out=w_raw[:], in_=skip_w.rearrange("(p j) n -> p j n", j=4))

        def load_vecs():
            nc.sync.dma_start(out=gw_bf[:], in_=gn_w.rearrange("(p t) -> p t", t=4))
            nc.sync.dma_start(out=gb_bf[:], in_=gn_b.rearrange("(p t) -> p t", t=4))
            nc.sync.dma_start(out=sb_bf[:], in_=skip_b.rearrange("(p t) -> p t", t=4))

        def load_d():
            nc.sync.dma_start(out=d_raw[:], in_=down_w.rearrange("(p j) n -> p j n", j=4))

        def load_db():
            nc.sync.dma_start(out=db4[:, 0, :], in_=down_b.partition_broadcast(P))

        def store(b):
            nc.sync.dma_start(out=out_v[b], in_=tiles["o", b][:])

        dmas = []
        for b in range(NBLK):
            dmas.append((JB * b - LA_ST, 0, load_h, b))
            dmas.append((JB * b - 11, 1, load_xc, b))
            dmas.append((JB * b - 3, 2, load_xr, b))
            dmas.append((JB * b, 3, load_x, b))
        dmas.append((-16, 0, load_w, None))
        dmas.append((-10, 0, load_vecs, None))
        dmas.append((-14, 5, load_d, None))
        dmas.append((-2, 4, load_db, None))
        dmas = sorted(dmas, key=lambda e: (e[0], e[1]))

        def g_groups(i):
            return 1 if i < JB else G_GROUPS[i % 2]

        def on_vector(b):
            return B_SWITCH <= b < B_BACK or b == NBLK - 1

        def on_scalar(i):
            return i % JB == JB - 1 and i < S_STAT_TILES

        def stats(i, a):
            beta, r = divmod(i, BT)
            if r == 0 and a == 0:
                tiles["st", beta] = work.tile([P, BT * 12], F32, name="st", tag="st", bufs=3)
            if on_scalar(i):
                return
            b, j = divmod(i, JB)
            src = tiles["h", b][:, j, 256 * a : 256 * (a + 1)].rearrange("p (g c) -> p c g", g=2)
            nc.vector.bn_stats(out=tiles["st", beta][:, 12 * r + 6 * a : 12 * r + 6 * a + 6], in_=src)

        def rstd_v(beta):
            t = work.tile([P, BT * 4], F32, name="rstd", tag="rstd", bufs=3)
            tiles["rstd", beta] = t
            nc.vector.reciprocal(out=t[:], in_=tiles["sd", beta][:])

        def quant_w():
            nc.vector.quantize_mx(out=w_codes[:].bitcast(FP8X4), scales=w_scales[:], in_=w_grp[:])

        def quant_d():
            nc.vector.quantize_mx(out=d_codes[:].bitcast(FP8X4), scales=d_scales[:], in_=d_grp[:])

        def vecs_v():
            nc.vector.tensor_copy(out=w32[:], in_=gw_bf[:])
            nc.vector.tensor_tensor(out=cb32[:], in0=gb_bf[:], in1=sb_bf[:], op=ALU.add)

        def db_v():
            for j in range(1, JB):
                nc.vector.tensor_copy(out=db4[:, j, :], in_=db4[:, 0, :])

        def quant_xc(b):
            c = work.tile([P, JB * P], U32, name="xc_codes", tag="xc_codes", bufs=2, align_bytes=64)
            s = work.tile([P, JB * P], U8, name="xc_scales", tag="xc_scales", bufs=2, align_bytes=64)
            tiles["xcq", b] = (c, s)
            nc.vector.quantize_mx(out=c[:].bitcast(FP8X4), scales=s[:], in_=tiles["xcg", b][:])

        def add_f(u):
            b, t = divmod(u, 4)
            if t == 0:
                tiles["f", b] = work.tile([P, JB, P // 4, 4, 4], F32, name="f_sum", tag="f_sum", bufs=2)
            nc.vector.tensor_tensor(
                out=tiles["f", b][:, :, :, t, :],
                in0=tiles["xsT", u][:].rearrange("p j (c i) -> p j c i", i=4),
                in1=tiles["hw", u][:].rearrange("p j (c i) -> p j c i", i=4),
                op=ALU.add,
            )

        def gate(i):
            b, j = divmod(i, JB)
            t = work.tile([P, 4 * P], BF16, name="g_bf", tag="g_bf", bufs=3, align_bytes=64)
            tiles["g", i] = t
            nc.vector.tensor_tensor(
                out=t[:].rearrange("p (c i t) -> p c t i", i=4, t=4),
                in0=tiles["f", b][:, j, :, :, :],
                in1=tiles["sT", i][:].rearrange("p t (c i) -> p c t i", i=4),
                op=ALU.mult,
            )

        def quant_g(i):
            c = work.tile([P, P], U32, name="g_codes", tag="g_codes", bufs=4, align_bytes=64)
            s = work.tile([P, P], U8, name="g_scales", tag="g_scales", bufs=4, align_bytes=64)
            tiles["gq", i] = (c, s)
            nc.vector.quantize_mx(out=c[:].bitcast(FP8X4), scales=s[:], in_=tiles["g", i][:])


        def preload_sqrt():
            nc.scalar.activation(out=warm[:, 1:2], in_=warm[:, 0:1], func=ACT.Sqrt)

        def stats_s(i):
            beta, r = divmod(i, BT)
            b, j = divmod(i, JB)
            st = tiles["st", beta]
            for sweep in range(2):
                for q in range(4):
                    col = 12 * r + 3 * q
                    junk = work.tile([P, P], BF16, name="junk", tag="junk", bufs=2)
                    src = tiles["h", b][:, j, P * q : P * (q + 1)]
                    if sweep == 0:
                        nc.scalar.activation(
                            out=junk[:], in_=src, func=ACT.Identity, scale=1.0 / P, accum_out=st[:, col + 1 : col + 2]
                        )
                    else:
                        nc.scalar.activation(
                            out=junk[:],
                            in_=src,
                            func=ACT.Square,
                            bias=st[:, col + 1 : col + 2],
                            scale=-1.0,
                            accum_out=st[:, col + 2 : col + 3],
                        )

        def sd_s(beta):
            t = work.tile([P, BT * 4], F32, name="sd", tag="sd", bufs=3)
            tiles["sd", beta] = t
            m2 = tiles["st", beta][:].rearrange("p (n c) -> p n c", c=3)[:, :, 2]
            nc.scalar.activation(out=t[:], in_=m2, func=ACT.Sqrt, bias=EPS, scale=1.0 / P)

        def silu(i):
            b, j = divmod(i, JB)
            t = work.tile([P, 4, P], F32, name="s_perm", tag="s_perm", bufs=4)
            tiles["sP", i] = t
            nc.scalar.activation(
                out=t[:], in_=tiles["xr", b][:, j, :].rearrange("p (c t) -> p t c", t=4), func=ACT.Silu
            )

        def normalise_s(i):
            b, j = divmod(i, JB)
            beta, r = divmod(i, BT)
            for q in range(g_groups(i), 4):
                col = 4 * r + q
                nc.scalar.activation(
                    out=tiles["hnP", i][:, :, 32 * q : 32 * (q + 1)],
                    in_=tiles["h", b][:, j, P * q : P * (q + 1)].rearrange("p (c t) -> p t c", t=4),
                    func=ACT.Identity,
                    bias=tiles["nmr", beta][:, col : col + 1],
                    scale=tiles["rstd", beta][:, col : col + 1],
                )

        def copy_xc(k):
            b, half = divmod(k, 2)
            if half == 0:
                tiles["xcg", b] = work.tile([P, JB * 4 * P], BF16, name="xc_grp", tag="xc_grp", bufs=2, align_bytes=64)
            nc.scalar.copy(
                out=tiles["xcg", b][:, 8 * P * half : 8 * P * (half + 1)].bitcast(F32).rearrange("p (r k u) -> p r k u", r=2, u=2),
                in_=tiles["xcT", k][:].rearrange("p r u k -> p r k u"),
            )

        def affine(u):
            t = u % 4
            hw = work.tile([P, JB, P], F32, name="hw", tag="hw", bufs=3)
            tiles["hw", u] = hw
            nc.scalar.activation(
                out=hw[:], in_=tiles["hnT", u][:], func=ACT.Identity, bias=cb32[:, t : t + 1], scale=w32[:, t : t + 1]
            )

        def epilogue_v(b):
            t = io.tile([P, JB, IN], F32, name="o_blk", tag="o_blk", bufs=3)
            tiles["o", b] = t
            nc.vector.tensor_tensor(out=t[:], in0=tiles["y", b][:], in1=tiles["xb", b][:], op=ALU.add)

        def copy_y(b):
            t = io.tile([P, JB, IN], F32, name="y_sb", tag="y_sb", bufs=3)
            tiles["ysb", b] = t
            nc.scalar.copy(out=t[:], in_=tiles["y", b][:])

        def group_w():
            nc.gpsimd.tensor_scalar(
                out=w_grp[:].rearrange("p (t m j) -> p t m j", t=4, j=4),
                in0=w_raw[:].rearrange("p j (m t) -> p t m j", t=4),
                scalar1=1.0,
                scalar2=0.0,
                op0=ALU.mult,
                op1=ALU.add,
            )

        def group_d():
            nc.gpsimd.tensor_scalar(
                out=d_grp[:].rearrange("p (o j) -> p o j", j=4),
                in0=d_raw[:].rearrange("p j o -> p o j"),
                scalar1=1.0,
                scalar2=0.0,
                op0=ALU.mult,
                op1=ALU.add,
            )

        def epilogue(b):
            t = io.tile([P, JB, IN], F32, name="o_blk", tag="o_blk", bufs=3)
            tiles["o", b] = t
            nc.gpsimd.tensor_tensor(out=t[:], in0=tiles["ysb", b][:], in1=tiles["xb", b][:], op=ALU.add)

        def negmu_g(beta):
            t = work.tile([P, BT * 4], F32, name="negmu", tag="negmu", bufs=3)
            tiles["negmu", beta] = t
            mean = tiles["st", beta][:].rearrange("p (n c) -> p n c", c=3)[:, :, 1]
            nc.gpsimd.tensor_scalar(out=t[:], in0=mean, scalar1=-1.0, scalar2=0.0, op0=ALU.mult, op1=ALU.add)

        def normalise(i):
            b, j = divmod(i, JB)
            beta, r = divmod(i, BT)
            t = work.tile([P, 4, P], F32, name="hn_perm", tag="hn_perm", bufs=12)
            tiles["hnP", i] = t
            for q in range(g_groups(i)):
                col = 4 * r + q
                nc.gpsimd.tensor_scalar(
                    out=t[:, :, 32 * q : 32 * (q + 1)],
                    in0=tiles["h", b][:, j, P * q : P * (q + 1)].rearrange("p (c t) -> p t c", t=4),
                    scalar1=tiles["negmu", beta][:, col : col + 1],
                    scalar2=tiles["rstd", beta][:, col : col + 1],
                    op0=ALU.add,
                    op1=ALU.mult,
                )

        def nmr_g(beta):
            t = work.tile([P, BT * 4], F32, name="nmr", tag="nmr", bufs=3)
            tiles["nmr", beta] = t
            nc.gpsimd.tensor_tensor(out=t[:], in0=tiles["negmu", beta][:], in1=tiles["rstd", beta][:], op=ALU.mult)

        def residual(b):
            t = io.tile([P, JB, IN], F32, name="xb_blk", tag="xb_blk", bufs=3)
            tiles["xb", b] = t
            nc.gpsimd.tensor_tensor(out=t[:], in0=tiles["x", b][:], in1=db4[:], op=ALU.add)

        def transpose_xc(k):
            t = ps1.tile([P, 2, 2, P], F32, name="xcT", tag="xcT")
            tiles["xcT", k] = t
            for r in range(2):
                b, j = divmod(2 * k + r, JB)
                words = tiles["xc", b][:, j, :].bitcast(F32)
                for u in range(2):
                    nc.tensor.transpose(t[:, r, u, :], words[:, u::2], ident[:])

        def transpose_hn(u):
            b, t = divmod(u, 4)
            bank = ps2.tile([P, JB, P], F32, name="hnT", tag="hnT")
            tiles["hnT", u] = bank
            for j in range(JB):
                nc.tensor.transpose(bank[:, j, :], tiles["hnP", JB * b + j][:, t, :], ident[:])

        def transpose_s(i):
            t = ps2.tile([P, 4, P], F32, name="sT", tag="sT")
            tiles["sT", i] = t
            for q in range(4):
                nc.tensor.transpose(t[:, q, :], tiles["sP", i][:, q, :], ident[:])

        def matmul_1(u):
            b, t = divmod(u, 4)
            bank = ps2.tile([P, JB, P], BANK_DT, name="xsT", tag="xsT")
            tiles["xsT", u] = bank
            c, s = tiles["xcq", b]
            nc.tensor.matmul_mx(
                out=bank[:].rearrange("p j k -> p (j k)"),
                lhsT=w_codes[:, P * t : P * (t + 1)].bitcast(FP8X4),
                lhsT_scale=w_scales[:, P * t : P * (t + 1)],
                rhs=c[:].bitcast(FP8X4),
                rhs_scale=s[:],
                start=True,
                stop=True,
            )

        def matmul_2(i):
            b, j = divmod(i, JB)
            if j == 0:
                tiles["y", b] = ps1.tile([P, JB, IN], F32, name="y", tag="y")
            c, s = tiles["gq", i]
            nc.tensor.matmul_mx(
                out=tiles["y", b][:, j, :],
                lhsT=c[:].bitcast(FP8X4),
                lhsT_scale=s[:],
                rhs=d_codes[:].bitcast(FP8X4),
                rhs_scale=d_scales[:],
                start=True,
                stop=True,
            )

        def tile_ok(i):
            return 0 <= i < NT

        def due(slot, period, count):
            n, rest = divmod(slot, period)
            return n if rest == 0 and 0 <= n < count else None

        nc.gpsimd.memset(warm[:, 0:1], 1.0)
        preload_sqrt()
        make_identity(nc, ident[:])
        n_dma = 0
        for s in range(FIRST_SLOT, LAST_SLOT + 1):
            while n_dma < len(dmas) and dmas[n_dma][0] - LEAD <= s:
                e = dmas[n_dma]
                if e[3] is None:
                    e[2]()
                else:
                    e[2](e[3])
                n_dma += 1
            b = due(s - 8, JB, NBLK)
            if b is not None:
                store(b)

            if tile_ok(s):
                gate(s)
            if tile_ok(s + LA_ST):
                stats(s + LA_ST, 0)
            b = due(s - 5, JB, NBLK)
            if b is not None and on_vector(b):
                epilogue_v(b)
            if tile_ok(s + 4):
                add_f(s + 4)
            if s == -10:
                quant_w()
            if s == -9:
                vecs_v()
            if s == -4:
                quant_d()
            if s == -3:
                db_v()
            b = due(s + 7, JB, NBLK)
            if b is not None:
                quant_xc(b)
            beta = due(s + O_NORM + 1, BT, NBATCH)
            if beta is not None:
                rstd_v(beta)
            if tile_ok(s + LA_ST):
                stats(s + LA_ST, 1)
            if tile_ok(s):
                quant_g(s)

            if tile_ok(s + LA_ST) and on_scalar(s + LA_ST):
                stats_s(s + LA_ST)
            if tile_ok(s + 5):
                affine(s + 5)
            k = due(s + 10, 2, NPAIR)
            if k is not None:
                copy_xc(k)
            beta = due(s + O_NORM + 2, BT, NBATCH)
            if beta is not None:
                sd_s(beta)
            if tile_ok(s + O_NORM - 1):
                normalise_s(s + O_NORM - 1)
            if tile_ok(s + 3):
                silu(s + 3)
            b = due(s - 5, JB, NBLK)
            if b is not None and not on_vector(b):
                copy_y(b)

            if s == -15:
                group_w()
            if s == -14:
                group_d()
            b = due(s - 6, JB, NBLK)
            if b is not None and not on_vector(b):
                epilogue(b)
            if beta is not None:
                negmu_g(beta)
            beta = due(s + O_NORM + 1, BT, NBATCH)
            if beta is not None:
                nmr_g(beta)
            if tile_ok(s + O_NORM):
                normalise(s + O_NORM)
            b = due(s, JB, NBLK)
            if b is not None:
                residual(b)

            if tile_ok(s + 6):
                transpose_hn(s + 6)
            k = due(s + 11, 2, NPAIR)
            if k is not None:
                transpose_xc(k)
            if tile_ok(s + 1):
                transpose_s(s + 1)
            if tile_ok(s + 5):
                matmul_1(s + 5)
            if tile_ok(s - 2) and (s - 2) % JB == 0:
                matmul_2(s - 2)
            if tile_ok(s - 1) and (s - 1) % JB != 0:
                matmul_2(s - 1)
